import numpy as np
import ml_dtypes


def mxq(x, axis, fmt="e4m3"):
    dtype, down = {"e4m3": (ml_dtypes.float8_e4m3fn, 7), "e5m2": (ml_dtypes.float8_e5m2, 14)}[fmt]
    v = np.moveaxis(np.asarray(x, np.float32).astype(ml_dtypes.bfloat16).astype(np.float64), axis, -1)
    blocks = v.reshape(v.shape[:-1] + (-1, 32))
    amax = np.abs(blocks).max(-1, keepdims=True)
    byte = np.maximum(np.where(amax > 0, np.frexp(amax)[1] - 1 + 127, 0) - down, 1)
    scale = np.exp2(byte - 127.0)
    codes = (blocks / scale).astype(np.float32).astype(dtype).astype(np.float64)
    return np.moveaxis((codes * scale).reshape(v.shape), -1, axis)


WIDE = False


def mx_kscale(k):
    if not WIDE:
        return np.ones(k)
    levels = np.array([10, -10, 5, -5, 0])
    if k % 512:
        return np.exp2(np.random.permutation(np.resize(levels, k // 32))).repeat(32)
    a = np.empty((k // 512, 16))
    for p in range(k // 512):
        a[p, :8] = np.random.permutation(np.resize(levels, 8))
        for g in range(8):
            far = levels[np.abs(levels - a[p, g]) >= 10]
            a[p, g + 8] = far[np.random.randint(len(far))]
    return np.exp2(a.ravel()).repeat(32)


BF16 = ml_dtypes.bfloat16


def bf(x):
    return np.asarray(x, np.float32).astype(BF16)


def f64(x):
    return np.asarray(x).astype(np.float64)


B, T, D, H, G, HD, W = 1, 8192, 512, 2, 1, 128, 256
EPS = 1e-6


def rmsnorm(u, w):
    var = np.mean(u * u, axis=-1, keepdims=True)
    return u * (1.0 / np.sqrt(var + EPS)) * (1.0 + w)


def setup_inputs():
    s = mx_kscale(D)
    return {"x": bf(np.random.standard_normal((B, T, D)) * s),
            "Wq": bf(np.random.standard_normal((D, H * HD)) * 0.005 / np.sqrt(D) / s[:, None]),
            "Wk": bf(np.random.standard_normal((D, G * HD)) * 0.005 / np.sqrt(D) / s[:, None]),
            "Wv": bf(np.random.standard_normal((D, G * HD)) * 1.0 / np.sqrt(D) / s[:, None]),
            "q_scale": bf(np.random.standard_normal(HD) * 0.2),
            "k_scale": bf(np.random.standard_normal(HD) * 0.2)}


def reference(x, Wq, Wk, Wv, q_scale, k_scale):
    xq = mxq(f64(x), 2, "e4m3")
    q = (xq @ mxq(f64(Wq), 0, "e4m3")).reshape(B, T, H, HD).transpose(0, 2, 1, 3)
    k = (xq @ mxq(f64(Wk), 0, "e4m3")).reshape(B, T, G, HD).transpose(0, 2, 1, 3)
    v = (xq @ mxq(f64(Wv), 0, "e4m3")).reshape(B, T, G, HD).transpose(0, 2, 1, 3)
    return rmsnorm(q, f64(q_scale)), rmsnorm(k, f64(k_scale)), v

@@ -1,0 +1,236 @@
+from contextlib import ExitStack
+
+import concourse.mybir as mybir
+from concourse.masks import make_identity
+
+F32 = mybir.dt.float32
+BF16 = mybir.dt.bfloat16
+U32 = mybir.dt.uint32
+U8 = mybir.dt.uint8
+FP8X4 = mybir.dt.float8_e4m3fn_x4
+ACT = mybir.ActivationFunctionType
+ALU = mybir.AluOpType
+
+P = 128
+TOKENS = 8192
+K = 512
+PACK = 4
+HD = 128
+HEADS = 4
+NORMED = 3
+N_OUT = HEADS * HD
+EPS = 1e-6
+
+TILES = TOKENS // P
+UNIT = 2
+UNITS = TILES // UNIT
+LOAD_TILES = 8
+STORE_TILES = 8
+
+FLOPS = 2 * TOKENS * K * N_OUT
+
+
+def tile_groupedqueryattention_pa_t_kernel(
+    tc, x, Wq, Wk, Wv, q_scale, k_scale, out_0, out_1, out_2
+):
+    nc = tc.nc
+    with ExitStack() as ctx:
+        ctx.enter_context(tc.manual_schedule())
+        consts = ctx.enter_context(tc.tile_pool(name="consts", bufs=1))
+        xin = ctx.enter_context(tc.tile_pool(name="xin", bufs=1))
+        work = ctx.enter_context(tc.tile_pool(name="work", bufs=3))
+        stages = ctx.enter_context(tc.tile_pool(name="stages", bufs=6))
+        psum_xt = ctx.enter_context(tc.psum_pool(name="psum_xt", bufs=2))
+        psum_acc = ctx.enter_context(tc.psum_pool(name="psum_acc", bufs=6))
+
+        w_raws = []
+        for w_dram, w_cols in ((Wq, 2 * HD), (Wk, HD), (Wv, HD)):
+            w_raw = consts.tile([P, PACK, w_cols], BF16, name="w_raw%d" % len(w_raws))
+            nc.sync.dma_start(
+                out=w_raw[:], in_=w_dram.rearrange("(p t) c -> p t c", t=PACK)
+            )
+            w_raws.append(w_raw)
+
+        x_view = x.flatten_outer_dims().rearrange("(p j) k -> p j k", p=P)
+        load_sizes = [UNIT] * (LOAD_TILES // UNIT) + [LOAD_TILES] * (TILES // LOAD_TILES - 1)
+        x_words = []
+        for size in load_sizes:
+            j0 = len(x_words)
+            x_chunk = xin.tile([P, size, K], BF16, name="x_chunk%d" % j0)
+            nc.sync.dma_start(out=x_chunk[:], in_=x_view[:, j0 : j0 + size, :])
+            for j in range(size):
+                x_words.append(x_chunk[:, j, :].bitcast(F32))
+
+        eps = consts.tile([P, 1], F32)
+        nc.vector.memset(eps[:], EPS)
+        ones = consts.tile([P, P], BF16)
+        nc.vector.memset(ones[:], 1.0)
+        gain_rows = consts.tile([P, 2 * HD], BF16)
+        nc.vector.memset(gain_rows[:], 0.0)
+        nc.scalar.dma_start(out=gain_rows[0:1, 0:HD], in_=q_scale.rearrange("(o d) -> o d", o=1))
+        nc.scalar.dma_start(
+            out=gain_rows[0:1, HD : 2 * HD], in_=k_scale.rearrange("(o d) -> o d", o=1)
+        )
+        warm = consts.tile([P, 1], F32)
+        nc.scalar.activation(out=warm[:], in_=eps[:], func=ACT.Abs_reciprocal_sqrt)
+        ident = consts.tile([P, P], F32)
+        make_identity(nc, ident[:])
+
+        w_grouped = consts.tile([P, N_OUT, PACK], BF16, align_bytes=64)
+        nc.vector.tensor_copy(
+            out=w_grouped[:, 0 : 2 * HD, :], in_=w_raws[0][:].rearrange("p t c -> p c t")
+        )
+        nc.scalar.copy(
+            out=w_grouped[:, 2 * HD : 3 * HD, :], in_=w_raws[1][:].rearrange("p t c -> p c t")
+        )
+        nc.scalar.copy(
+            out=w_grouped[:, 3 * HD : 4 * HD, :], in_=w_raws[2][:].rearrange("p t c -> p c t")
+        )
+        w_codes = consts.tile([P, N_OUT], U32, align_bytes=64)
+        w_scales = consts.tile([P, N_OUT], U8, align_bytes=64)
+        nc.vector.quantize_mx(
+            out=w_codes[:].bitcast(FP8X4),
+            scales=w_scales[:],
+            in_=w_grouped[:].rearrange("p c t -> p (c t)"),
+        )
+
+        gain = consts.tile([P, 2 * HD], F32)
+
+        def spread_gains():
+            gain_ps = psum_acc.tile([P, N_OUT], F32, tag="acc")
+            nc.tensor.matmul(
+                out=gain_ps[:, 0 : 2 * HD], lhsT=ones[:], rhs=gain_rows[:], start=True, stop=True
+            )
+            nc.vector.tensor_scalar_add(out=gain[:], in0=gain_ps[:, 0 : 2 * HD], scalar1=1.0)
+
+        out_views = [
+            out_0.flatten_outer_dims().rearrange("(h p j) d -> h p j d", h=2, p=P)[0],
+            out_0.flatten_outer_dims().rearrange("(h p j) d -> h p j d", h=2, p=P)[1],
+            out_1.flatten_outer_dims().rearrange("(p j) d -> p j d", p=P),
+            out_2.flatten_outer_dims().rearrange("(p j) d -> p j d", p=P),
+        ]
+
+        live = {}
+
+        def transposes(u):
+            xt = psum_xt.tile([P, UNIT, 2, P], F32)
+            for i in range(UNIT):
+                for half in range(2):
+                    nc.tensor.transpose(
+                        xt[:, i, half, :],
+                        x_words[u * UNIT + i][:, half : 2 * P : 2],
+                        ident[:],
+                    )
+            live["xt", u] = xt
+
+        def copy_out(u):
+            grouped = work.tile([P, UNIT * P * PACK], BF16, align_bytes=64)
+            interleaved = grouped[:].bitcast(F32).rearrange("p (i n h) -> p i n h", i=UNIT, h=2)
+            planes = live["xt", u][:].rearrange("p i h n -> p i n h")
+            nc.scalar.copy(out=interleaved, in_=planes)
+            live["grouped", u] = grouped
+
+        def quantise(u):
+            codes = work.tile([P, UNIT * P], U32, align_bytes=64)
+            scales = work.tile([P, UNIT * P], U8, align_bytes=64)
+            nc.vector.quantize_mx(
+                out=codes[:].bitcast(FP8X4), scales=scales[:], in_=live["grouped", u][:]
+            )
+            live["codes", u] = (codes, scales)
+
+        def project(u):
+            codes, scales = live["codes", u]
+            accs = []
+            for i in range(UNIT):
+                acc = psum_acc.tile([P, N_OUT], F32, tag="acc")
+                nc.tensor.matmul_mx(
+                    out=acc[:],
+                    lhsT=codes[:, i * P : (i + 1) * P].bitcast(FP8X4),
+                    lhsT_scale=scales[:, i * P : (i + 1) * P],
+                    rhs=w_codes[:].bitcast(FP8X4),
+                    rhs_scale=w_scales[:],
+                    start=True,
+                    stop=True,
+                )
+                accs.append(acc)
+            live["accs", u] = accs
+
+        def squares(u):
+            squared = work.tile([P, UNIT * NORMED, HD], F32)
+            sums = work.tile([P, UNIT * NORMED], F32)
+            for i in range(UNIT):
+                for h in range(NORMED):
+                    c = i * NORMED + h
+                    nc.scalar.activation(
+                        out=squared[:, c, :],
+                        in_=live["accs", u][i][:, h * HD : (h + 1) * HD],
+                        func=ACT.Square,
+                        accum_out=sums[:, c : c + 1],
+                    )
+            live["sums", u] = sums
+
+        def inverse_rms(u):
+            rstd = work.tile([P, UNIT * NORMED], F32)
+            nc.scalar.activation(
+                out=rstd[:],
+                in_=live["sums", u][:],
+                func=ACT.Abs_reciprocal_sqrt,
+                scale=1.0 / HD,
+                bias=eps[:],
+            )
+            live["rstd", u] = rstd
+
+        def write_out(u):
+            first_tile = u * UNIT
+            if first_tile % STORE_TILES == 0:
+                stage = stages.tile([P, HEADS, STORE_TILES, HD], F32)
+                live["stage"] = stage
+            stage = live["stage"]
+            rstd = live["rstd", u]
+            accs = live["accs", u]
+            for i in range(UNIT):
+                s = (first_tile + i) % STORE_TILES
+                for h in range(NORMED):
+                    c = i * NORMED + h
+                    g = h // 2
+                    nc.vector.scalar_tensor_tensor(
+                        out=stage[:, h, s, :],
+                        in0=accs[i][:, h * HD : (h + 1) * HD],
+                        scalar=rstd[:, c : c + 1],
+                        in1=gain[:, g * HD : (g + 1) * HD],
+                        op0=ALU.mult,
+                        op1=ALU.mult,
+                    )
+                nc.vector.tensor_copy(
+                    out=stage[:, NORMED, s, :], in_=accs[i][:, NORMED * HD : N_OUT]
+                )
+            if first_tile >= TILES - STORE_TILES:
+                stored = UNIT
+            elif (first_tile + UNIT) % STORE_TILES == 0:
+                stored = STORE_TILES
+            else:
+                stored = 0
+            if stored > 0:
+                j0 = first_tile + UNIT - stored
+                s0 = j0 % STORE_TILES
+                for h in range(HEADS):
+                    nc.sync.dma_start(
+                        out=out_views[h][:, j0 : j0 + stored, :], in_=stage[:, h, s0 : s0 + stored, :]
+                    )
+
+        for r in range(-2, UNITS + 1):
+            if r == 0:
+                spread_gains()
+            if 0 <= r + 2 < UNITS:
+                transposes(r + 2)
+            if 0 <= r + 1 < UNITS:
+                quantise(r + 1)
+                project(r + 1)
+            if 0 <= r < UNITS:
+                squares(r)
+            if 0 <= r + 2 < UNITS:
+                copy_out(r + 2)
+            if 0 <= r < UNITS:
+                inverse_rms(r)
+            if 0 <= r - 1 < UNITS:
+                write_out(r - 1)

@@ -18,6 +18,7 @@ PACK = 4
 HD = 128
 HEADS = 4
 NORMED = 3
+QUERIES = 2
 N_OUT = HEADS * HD
 EPS = 1e-6
 
@@ -156,21 +157,43 @@ def tile_groupedqueryattention_pa_t_kernel(
             live["accs", u] = accs
 
         def squares(u):
-            squared = work.tile([P, UNIT * NORMED, HD], F32)
-            sums = work.tile([P, UNIT * NORMED], F32)
+            squared = work.tile([P, UNIT * QUERIES, HD], F32)
+            sums = work.tile([P, UNIT, NORMED], F32)
             for i in range(UNIT):
-                for h in range(NORMED):
-                    c = i * NORMED + h
+                for h in range(QUERIES):
                     nc.scalar.activation(
-                        out=squared[:, c, :],
+                        out=squared[:, i * QUERIES + h, :],
                         in_=live["accs", u][i][:, h * HD : (h + 1) * HD],
                         func=ACT.Square,
-                        accum_out=sums[:, c : c + 1],
+                        accum_out=sums[:, i, h : h + 1],
                     )
             live["sums", u] = sums
 
+        def key_stats(u):
+            stats = work.tile([P, UNIT, 2, 3], F32)
+            for i in range(UNIT):
+                nc.vector.bn_stats(
+                    out=stats[:, i, :, :].rearrange("p e s -> p (e s)"),
+                    in_=live["accs", u][i][:, QUERIES * HD : NORMED * HD],
+                )
+            live["stats", u] = stats
+
+        def key_mean_squares(u):
+            means = live["stats", u][:].rearrange("p i e s -> p (i e) s")[:, :, 1]
+            nc.vector.scalar_tensor_tensor(
+                out=means, in0=means, scalar=HD / 2.0, in1=means, op0=ALU.mult, op1=ALU.mult
+            )
+
+        def key_sums(u):
+            nc.vector.tensor_reduce(
+                out=live["sums", u][:, :, QUERIES],
+                in_=live["stats", u][:, :, :, 1:3],
+                axis=mybir.AxisListType.XY,
+                op=ALU.add,
+            )
+
         def inverse_rms(u):
-            rstd = work.tile([P, UNIT * NORMED], F32)
+            rstd = work.tile([P, UNIT, NORMED], F32)
             nc.scalar.activation(
                 out=rstd[:],
                 in_=live["sums", u][:],
@@ -180,30 +203,35 @@ def tile_groupedqueryattention_pa_t_kernel(
             )
             live["rstd", u] = rstd
 
-        def write_out(u):
-            first_tile = u * UNIT
-            if first_tile % STORE_TILES == 0:
+        def stage_of(u):
+            key = ("stage", u * UNIT // STORE_TILES)
+            if key not in live:
                 stage = stages.tile([P, HEADS, STORE_TILES, HD], F32)
-                live["stage"] = stage
-            stage = live["stage"]
-            rstd = live["rstd", u]
-            accs = live["accs", u]
+                live[key] = stage
+            return live[key]
+
+        def values_out(u):
             for i in range(UNIT):
-                s = (first_tile + i) % STORE_TILES
-                for h in range(NORMED):
-                    c = i * NORMED + h
-                    g = h // 2
-                    nc.vector.scalar_tensor_tensor(
-                        out=stage[:, h, s, :],
-                        in0=accs[i][:, h * HD : (h + 1) * HD],
-                        scalar=rstd[:, c : c + 1],
-                        in1=gain[:, g * HD : (g + 1) * HD],
-                        op0=ALU.mult,
-                        op1=ALU.mult,
-                    )
-                nc.vector.tensor_copy(
-                    out=stage[:, NORMED, s, :], in_=accs[i][:, NORMED * HD : N_OUT]
+                s = (u * UNIT + i) % STORE_TILES
+                nc.scalar.copy(
+                    out=stage_of(u)[:, NORMED, s, :],
+                    in_=live["accs", u][i][:, NORMED * HD : N_OUT],
                 )
+
+        def normed_out(u, i, h):
+            s = (u * UNIT + i) % STORE_TILES
+            g = h // 2
+            nc.vector.scalar_tensor_tensor(
+                out=stage_of(u)[:, h, s, :],
+                in0=live["accs", u][i][:, h * HD : (h + 1) * HD],
+                scalar=live["rstd", u][:, i, h : h + 1],
+                in1=gain[:, g * HD : (g + 1) * HD],
+                op0=ALU.mult,
+                op1=ALU.mult,
+            )
+
+        def store(u):
+            first_tile = u * UNIT
             if first_tile >= TILES - STORE_TILES:
                 stored = UNIT
             elif (first_tile + UNIT) % STORE_TILES == 0:
@@ -215,7 +243,8 @@ def tile_groupedqueryattention_pa_t_kernel(
                 s0 = j0 % STORE_TILES
                 for h in range(HEADS):
                     nc.sync.dma_start(
-                        out=out_views[h][:, j0 : j0 + stored, :], in_=stage[:, h, s0 : s0 + stored, :]
+                        out=out_views[h][:, j0 : j0 + stored, :],
+                        in_=stage_of(u)[:, h, s0 : s0 + stored, :],
                     )
 
         for r in range(-2, UNITS + 1):
@@ -226,11 +255,27 @@ def tile_groupedqueryattention_pa_t_kernel(
             if 0 <= r + 1 < UNITS:
                 quantise(r + 1)
                 project(r + 1)
-            if 0 <= r < UNITS:
+            this = 0 <= r < UNITS
+            last = 0 <= r - 1 < UNITS
+            if this:
                 squares(r)
             if 0 <= r + 2 < UNITS:
                 copy_out(r + 2)
-            if 0 <= r < UNITS:
+            if last:
+                for h in range(NORMED):
+                    normed_out(r - 1, 0, h)
+            if this:
+                key_stats(r)
+                values_out(r)
+            if last:
+                normed_out(r - 1, 1, 0)
+            if this:
+                key_mean_squares(r)
+            if last:
+                normed_out(r - 1, 1, 1)
+            if this:
+                key_sums(r)
                 inverse_rms(r)
-            if 0 <= r - 1 < UNITS:
-                write_out(r - 1)
+            if last:
+                normed_out(r - 1, 1, 2)
+                store(r - 1)

@@ -42,7 +42,7 @@ def tile_groupedqueryattention_pa_t_kernel(
         work = ctx.enter_context(tc.tile_pool(name="work", bufs=3))
         stages = ctx.enter_context(tc.tile_pool(name="stages", bufs=6))
         psum_xt = ctx.enter_context(tc.psum_pool(name="psum_xt", bufs=2))
-        psum_acc = ctx.enter_context(tc.psum_pool(name="psum_acc", bufs=6))
+        psum_acc = ctx.enter_context(tc.psum_pool(name="psum_acc", bufs=3))
 
         w_raws = []
         for w_dram, w_cols in ((Wq, 2 * HD), (Wk, HD), (Wv, HD)):
@@ -98,7 +98,7 @@ def tile_groupedqueryattention_pa_t_kernel(
         gain = consts.tile([P, 2 * HD], F32)
 
         def spread_gains():
-            gain_ps = psum_acc.tile([P, N_OUT], F32, tag="acc")
+            gain_ps = psum_acc.tile([P, N_OUT], F32, tag="kv")
             nc.tensor.matmul(
                 out=gain_ps[:, 0 : 2 * HD], lhsT=ones[:], rhs=gain_rows[:], start=True, stop=True
             )
@@ -141,20 +141,27 @@ def tile_groupedqueryattention_pa_t_kernel(
 
         def project(u):
             codes, scales = live["codes", u]
-            accs = []
-            for i in range(UNIT):
-                acc = psum_acc.tile([P, N_OUT], F32, tag="acc")
+            queries = psum_acc.tile([P, UNIT, QUERIES, HD], F32, tag="q")
+            keyvals = psum_acc.tile([P, 2, UNIT, HD], F32, tag="kv")
+
+            def multiply(out, i, first_col, cols):
                 nc.tensor.matmul_mx(
-                    out=acc[:],
+                    out=out,
                     lhsT=codes[:, i * P : (i + 1) * P].bitcast(FP8X4),
                     lhsT_scale=scales[:, i * P : (i + 1) * P],
-                    rhs=w_codes[:].bitcast(FP8X4),
-                    rhs_scale=w_scales[:],
+                    rhs=w_codes[:, first_col : first_col + cols].bitcast(FP8X4),
+                    rhs_scale=w_scales[:, first_col : first_col + cols],
                     start=True,
                     stop=True,
                 )
-                accs.append(acc)
-            live["accs", u] = accs
+
+            for i in range(UNIT):
+                multiply(queries[:, i, :, :].rearrange("p h d -> p (h d)"), i, 0, QUERIES * HD)
+            for i in range(UNIT):
+                for g in range(2):
+                    multiply(keyvals[:, g, i, :], i, (QUERIES + g) * HD, HD)
+            live["queries", u] = queries
+            live["keyvals", u] = keyvals
 
         def squares(u):
             squared = work.tile([P, UNIT * QUERIES, HD], F32)
@@ -163,7 +170,7 @@ def tile_groupedqueryattention_pa_t_kernel(
                 for h in range(QUERIES):
                     nc.scalar.activation(
                         out=squared[:, i * QUERIES + h, :],
-                        in_=live["accs", u][i][:, h * HD : (h + 1) * HD],
+                        in_=live["queries", u][:, i, h, :],
                         func=ACT.Square,
                         accum_out=sums[:, i, h : h + 1],
                     )
@@ -174,7 +181,7 @@ def tile_groupedqueryattention_pa_t_kernel(
             for i in range(UNIT):
                 nc.vector.bn_stats(
                     out=stats[:, i, :, :].rearrange("p e s -> p (e s)"),
-                    in_=live["accs", u][i][:, QUERIES * HD : NORMED * HD],
+                    in_=live["keyvals", u][:, 0, i, :],
                 )
             live["stats", u] = stats
 
@@ -211,19 +218,20 @@ def tile_groupedqueryattention_pa_t_kernel(
             return live[key]
 
         def values_out(u):
-            for i in range(UNIT):
-                s = (u * UNIT + i) % STORE_TILES
-                nc.scalar.copy(
-                    out=stage_of(u)[:, NORMED, s, :],
-                    in_=live["accs", u][i][:, NORMED * HD : N_OUT],
-                )
+            s = u * UNIT % STORE_TILES
+            nc.scalar.copy(
+                out=stage_of(u)[:, NORMED, s : s + UNIT, :], in_=live["keyvals", u][:, 1, :, :]
+            )
 
         def normed_out(u, i, h):
             s = (u * UNIT + i) % STORE_TILES
-            g = h // 2
+            if h < QUERIES:
+                projected, g = live["queries", u][:, i, h, :], 0
+            else:
+                projected, g = live["keyvals", u][:, 0, i, :], 1
             nc.vector.scalar_tensor_tensor(
                 out=stage_of(u)[:, h, s, :],
-                in0=live["accs", u][i][:, h * HD : (h + 1) * HD],
+                in0=projected,
                 scalar=live["rstd", u][:, i, h : h + 1],
                 in1=gain[:, g * HD : (g + 1) * HD],
                 op0=ALU.mult,
@@ -247,35 +255,34 @@ def tile_groupedqueryattention_pa_t_kernel(
                         in_=stage_of(u)[:, h, s0 : s0 + stored, :],
                     )
 
-        for r in range(-2, UNITS + 1):
+        for r in range(-3, UNITS + 1):
+            this = 0 <= r < UNITS
+            last = 0 <= r - 1 < UNITS
             if r == 0:
                 spread_gains()
+            if 0 <= r + 3 < UNITS:
+                transposes(r + 3)
             if 0 <= r + 2 < UNITS:
-                transposes(r + 2)
+                copy_out(r + 2)
             if 0 <= r + 1 < UNITS:
                 quantise(r + 1)
                 project(r + 1)
-            this = 0 <= r < UNITS
-            last = 0 <= r - 1 < UNITS
             if this:
                 squares(r)
-            if 0 <= r + 2 < UNITS:
-                copy_out(r + 2)
-            if last:
-                for h in range(NORMED):
-                    normed_out(r - 1, 0, h)
-            if this:
                 key_stats(r)
                 values_out(r)
             if last:
-                normed_out(r - 1, 1, 0)
+                for i in range(UNIT):
+                    normed_out(r - 1, 0, i)
             if this:
                 key_mean_squares(r)
             if last:
-                normed_out(r - 1, 1, 1)
+                for i in range(UNIT):
+                    normed_out(r - 1, 1, i)
             if this:
                 key_sums(r)
                 inverse_rms(r)
             if last:
-                normed_out(r - 1, 1, 2)
+                for i in range(UNIT):
+                    normed_out(r - 1, i, QUERIES)
                 store(r - 1)

@@ -240,14 +240,14 @@ def tile_groupedqueryattention_pa_t_kernel(
 
         def store(u):
             first_tile = u * UNIT
+            stored = STORE_TILES
+            if first_tile >= TILES - 2 * STORE_TILES:
+                stored = STORE_TILES // 2
             if first_tile >= TILES - STORE_TILES:
                 stored = UNIT
-            elif (first_tile + UNIT) % STORE_TILES == 0:
-                stored = STORE_TILES
-            else:
-                stored = 0
-            if stored > 0:
-                j0 = first_tile + UNIT - stored
+            end_tile = first_tile + UNIT
+            if end_tile % stored == 0:
+                j0 = end_tile - stored
                 s0 = j0 % STORE_TILES
                 for h in range(HEADS):
                     nc.sync.dma_start(

@@ -25,6 +25,8 @@ EPS = 1e-6
 TILES = TOKENS // P
 UNIT = 2
 UNITS = TILES // UNIT
+WARM_COLS = 256
+WARM_UP = 10
 LOAD_TILES = 8
 STORE_TILES = 8
 
@@ -64,7 +66,7 @@ def tile_groupedqueryattention_pa_t_kernel(
 
         eps = consts.tile([P, 1], F32)
         nc.vector.memset(eps[:], EPS)
-        ones = consts.tile([P, P], BF16)
+        ones = consts.tile([P, WARM_COLS], BF16)
         nc.vector.memset(ones[:], 1.0)
         gain_rows = consts.tile([P, 2 * HD], BF16)
         nc.vector.memset(gain_rows[:], 0.0)
@@ -100,7 +102,7 @@ def tile_groupedqueryattention_pa_t_kernel(
         def spread_gains():
             gain_ps = psum_acc.tile([P, N_OUT], F32, tag="kv")
             nc.tensor.matmul(
-                out=gain_ps[:, 0 : 2 * HD], lhsT=ones[:], rhs=gain_rows[:], start=True, stop=True
+                out=gain_ps[:, 0 : 2 * HD], lhsT=ones[:, 0:P], rhs=gain_rows[:], start=True, stop=True
             )
             nc.vector.tensor_scalar_add(out=gain[:], in0=gain_ps[:, 0 : 2 * HD], scalar1=1.0)
 
@@ -111,10 +113,21 @@ def tile_groupedqueryattention_pa_t_kernel(
             out_2.flatten_outer_dims().rearrange("(p j) d -> p j d", p=P),
         ]
 
+        def keep_warm(xt):
+            nc.tensor.matmul(
+                out=xt[:].rearrange("p i h n -> p (i h n)")[:, 0:WARM_COLS],
+                lhsT=ones[:, 0:P],
+                rhs=ones[:],
+                start=True,
+                stop=True,
+            )
+
         live = {}
 
         def transposes(u):
             xt = psum_xt.tile([P, UNIT, 2, P], F32)
+            for n in range(WARM_UP if u == 0 else 1):
+                keep_warm(xt)
             for i in range(UNIT):
                 for half in range(2):
                     nc.tensor.transpose(

@@ -24,7 +24,9 @@ EPS = 1e-6
 
 TILES = TOKENS // P
 UNIT = 2
-UNITS = TILES // UNIT
+SINGLES = 2
+UNIT_STARTS = list(range(0, TILES - SINGLES, UNIT)) + list(range(TILES - SINGLES, TILES))
+UNITS = len(UNIT_STARTS)
 WARM_COLS = 256
 WARM_UP = 10
 LOAD_TILES = 8
@@ -46,23 +48,27 @@ def tile_groupedqueryattention_pa_t_kernel(
         psum_xt = ctx.enter_context(tc.psum_pool(name="psum_xt", bufs=2))
         psum_acc = ctx.enter_context(tc.psum_pool(name="psum_acc", bufs=3))
 
-        w_raws = []
-        for w_dram, w_cols in ((Wq, 2 * HD), (Wk, HD), (Wv, HD)):
-            w_raw = consts.tile([P, PACK, w_cols], BF16, name="w_raw%d" % len(w_raws))
-            nc.sync.dma_start(
-                out=w_raw[:], in_=w_dram.rearrange("(p t) c -> p t c", t=PACK)
-            )
-            w_raws.append(w_raw)
+        def load_weight(w_dram, cols, name):
+            w_raw = consts.tile([P, PACK, cols], BF16, name=name)
+            nc.sync.dma_start(out=w_raw[:], in_=w_dram.rearrange("(p t) c -> p t c", t=PACK))
+            return w_raw
 
         x_view = x.flatten_outer_dims().rearrange("(p j) k -> p j k", p=P)
-        load_sizes = [UNIT] * (LOAD_TILES // UNIT) + [LOAD_TILES] * (TILES // LOAD_TILES - 1)
         x_words = []
-        for size in load_sizes:
+
+        def load_x(size):
             j0 = len(x_words)
             x_chunk = xin.tile([P, size, K], BF16, name="x_chunk%d" % j0)
             nc.sync.dma_start(out=x_chunk[:], in_=x_view[:, j0 : j0 + size, :])
             for j in range(size):
                 x_words.append(x_chunk[:, j, :].bitcast(F32))
+
+        wq_raw = load_weight(Wq, QUERIES * HD, "wq_raw")
+        load_x(UNIT)
+        wk_raw = load_weight(Wk, HD, "wk_raw")
+        wv_raw = load_weight(Wv, HD, "wv_raw")
+        for size in [UNIT] * (LOAD_TILES // UNIT - 1) + [LOAD_TILES] * (TILES // LOAD_TILES - 1):
+            load_x(size)
 
         eps = consts.tile([P, 1], F32)
         nc.vector.memset(eps[:], EPS)
@@ -80,22 +86,29 @@ def tile_groupedqueryattention_pa_t_kernel(
         make_identity(nc, ident[:])
 
         w_grouped = consts.tile([P, N_OUT, PACK], BF16, align_bytes=64)
-        nc.vector.tensor_copy(
-            out=w_grouped[:, 0 : 2 * HD, :], in_=w_raws[0][:].rearrange("p t c -> p c t")
-        )
-        nc.scalar.copy(
-            out=w_grouped[:, 2 * HD : 3 * HD, :], in_=w_raws[1][:].rearrange("p t c -> p c t")
-        )
-        nc.scalar.copy(
-            out=w_grouped[:, 3 * HD : 4 * HD, :], in_=w_raws[2][:].rearrange("p t c -> p c t")
-        )
         w_codes = consts.tile([P, N_OUT], U32, align_bytes=64)
         w_scales = consts.tile([P, N_OUT], U8, align_bytes=64)
-        nc.vector.quantize_mx(
-            out=w_codes[:].bitcast(FP8X4),
-            scales=w_scales[:],
-            in_=w_grouped[:].rearrange("p c t -> p (c t)"),
-        )
+
+        def regroup(copy, w_raw, h):
+            first = h * HD if h < QUERIES else 0
+            copy(
+                out=w_grouped[:, h * HD : (h + 1) * HD, :],
+                in_=w_raw[:, :, first : first + HD].rearrange("p t c -> p c t"),
+            )
+
+        def quantise_weights(heads):
+            cols = slice(heads.start * HD, heads.stop * HD)
+            nc.vector.quantize_mx(
+                out=w_codes[:, cols].bitcast(FP8X4),
+                scales=w_scales[:, cols],
+                in_=w_grouped[:, cols, :].rearrange("p c t -> p (c t)"),
+            )
+
+        regroup(nc.vector.tensor_copy, wq_raw, 0)
+        regroup(nc.scalar.copy, wq_raw, 1)
+        regroup(nc.vector.tensor_copy, wk_raw, 2)
+        quantise_weights(slice(0, 2))
+        regroup(nc.vector.tensor_copy, wv_raw, 3)
 
         gain = consts.tile([P, 2 * HD], F32)
 
@@ -106,12 +119,17 @@ def tile_groupedqueryattention_pa_t_kernel(
             )
             nc.vector.tensor_scalar_add(out=gain[:], in0=gain_ps[:, 0 : 2 * HD], scalar1=1.0)
 
+        queries_out = out_0.flatten_outer_dims().rearrange("(h p j) d -> h p j d", h=2, p=P)
         out_views = [
-            out_0.flatten_outer_dims().rearrange("(h p j) d -> h p j d", h=2, p=P)[0],
-            out_0.flatten_outer_dims().rearrange("(h p j) d -> h p j d", h=2, p=P)[1],
-            out_1.flatten_outer_dims().rearrange("(p j) d -> p j d", p=P),
-            out_2.flatten_outer_dims().rearrange("(p j) d -> p j d", p=P),
+            (out_2.flatten_outer_dims().rearrange("(p j) d -> p j d", p=P), NORMED),
+            (queries_out[0], 0),
+            (queries_out[1], 1),
+            (out_1.flatten_outer_dims().rearrange("(p j) d -> p j d", p=P), QUERIES),
         ]
+
+        def tiles_of(u):
+            end = UNIT_STARTS[u + 1] if u + 1 < UNITS else TILES
+            return list(range(UNIT_STARTS[u], end))
 
         def keep_warm(xt):
             nc.tensor.matmul(
@@ -125,28 +143,26 @@ def tile_groupedqueryattention_pa_t_kernel(
         live = {}
 
         def transposes(u):
-            xt = psum_xt.tile([P, UNIT, 2, P], F32)
+            tiles = tiles_of(u)
+            xt = psum_xt.tile([P, len(tiles), 2, P], F32)
             for n in range(WARM_UP if u == 0 else 1):
                 keep_warm(xt)
-            for i in range(UNIT):
-                for half in range(2):
-                    nc.tensor.transpose(
-                        xt[:, i, half, :],
-                        x_words[u * UNIT + i][:, half : 2 * P : 2],
-                        ident[:],
-                    )
+            for i, t in enumerate(tiles):
+                for h in range(2):
+                    nc.tensor.transpose(xt[:, i, h, :], x_words[t][:, h : 2 * P : 2], ident[:])
             live["xt", u] = xt
 
         def copy_out(u):
-            grouped = work.tile([P, UNIT * P * PACK], BF16, align_bytes=64)
-            interleaved = grouped[:].bitcast(F32).rearrange("p (i n h) -> p i n h", i=UNIT, h=2)
-            planes = live["xt", u][:].rearrange("p i h n -> p i n h")
-            nc.scalar.copy(out=interleaved, in_=planes)
+            n_tiles = len(tiles_of(u))
+            grouped = work.tile([P, n_tiles * P * PACK], BF16, align_bytes=64)
+            interleaved = grouped[:].bitcast(F32).rearrange("p (i n h) -> p i n h", i=n_tiles, h=2)
+            nc.scalar.copy(out=interleaved, in_=live["xt", u][:].rearrange("p i h n -> p i n h"))
             live["grouped", u] = grouped
 
         def quantise(u):
-            codes = work.tile([P, UNIT * P], U32, align_bytes=64)
-            scales = work.tile([P, UNIT * P], U8, align_bytes=64)
+            cols = len(tiles_of(u)) * P
+            codes = work.tile([P, cols], U32, align_bytes=64)
+            scales = work.tile([P, cols], U8, align_bytes=64)
             nc.vector.quantize_mx(
                 out=codes[:].bitcast(FP8X4), scales=scales[:], in_=live["grouped", u][:]
             )
@@ -154,8 +170,9 @@ def tile_groupedqueryattention_pa_t_kernel(
 
         def project(u):
             codes, scales = live["codes", u]
-            queries = psum_acc.tile([P, UNIT, QUERIES, HD], F32, tag="q")
-            keyvals = psum_acc.tile([P, 2, UNIT, HD], F32, tag="kv")
+            n_tiles = len(tiles_of(u))
+            queries = psum_acc.tile([P, n_tiles, QUERIES, HD], F32, tag="q")
+            keyvals = psum_acc.tile([P, 2, n_tiles, HD], F32, tag="kv")
 
             def multiply(out, i, first_col, cols):
                 nc.tensor.matmul_mx(
@@ -168,33 +185,38 @@ def tile_groupedqueryattention_pa_t_kernel(
                     stop=True,
                 )
 
-            for i in range(UNIT):
+            for i in range(n_tiles):
                 multiply(queries[:, i, :, :].rearrange("p h d -> p (h d)"), i, 0, QUERIES * HD)
-            for i in range(UNIT):
+            for i in range(n_tiles):
                 for g in range(2):
                     multiply(keyvals[:, g, i, :], i, (QUERIES + g) * HD, HD)
             live["queries", u] = queries
             live["keyvals", u] = keyvals
 
-        def squares(u):
-            squared = work.tile([P, UNIT * QUERIES, HD], F32)
-            sums = work.tile([P, UNIT, NORMED], F32)
-            for i in range(UNIT):
-                for h in range(QUERIES):
+        def projected(u, i, h):
+            if h < QUERIES:
+                return live["queries", u][:, i, h, :]
+            return live["keyvals", u][:, h - QUERIES, i, :]
+
+        def squares(u, heads):
+            n_tiles = len(tiles_of(u))
+            squared = work.tile([P, n_tiles, len(heads), HD], F32)
+            for i in range(n_tiles):
+                for c, h in enumerate(heads):
                     nc.scalar.activation(
-                        out=squared[:, i * QUERIES + h, :],
-                        in_=live["queries", u][:, i, h, :],
+                        out=squared[:, i, c, :],
+                        in_=projected(u, i, h),
                         func=ACT.Square,
-                        accum_out=sums[:, i, h : h + 1],
+                        accum_out=live["sums", u][:, i, h : h + 1],
                     )
-            live["sums", u] = sums
 
         def key_stats(u):
-            stats = work.tile([P, UNIT, 2, 3], F32)
-            for i in range(UNIT):
+            n_tiles = len(tiles_of(u))
+            stats = work.tile([P, n_tiles, 2, 3], F32)
+            for i in range(n_tiles):
                 nc.vector.bn_stats(
                     out=stats[:, i, :, :].rearrange("p e s -> p (e s)"),
-                    in_=live["keyvals", u][:, 0, i, :],
+                    in_=projected(u, i, QUERIES),
                 )
             live["stats", u] = stats
 
@@ -213,7 +235,7 @@ def tile_groupedqueryattention_pa_t_kernel(
             )
 
         def inverse_rms(u):
-            rstd = work.tile([P, UNIT, NORMED], F32)
+            rstd = work.tile([P, len(tiles_of(u)), NORMED], F32)
             nc.scalar.activation(
                 out=rstd[:],
                 in_=live["sums", u][:],
@@ -223,28 +245,27 @@ def tile_groupedqueryattention_pa_t_kernel(
             )
             live["rstd", u] = rstd
 
-        def stage_of(u):
-            key = ("stage", u * UNIT // STORE_TILES)
+        def stage_of(t):
+            key = ("stage", t // STORE_TILES)
             if key not in live:
                 stage = stages.tile([P, HEADS, STORE_TILES, HD], F32)
                 live[key] = stage
             return live[key]
 
         def values_out(u):
-            s = u * UNIT % STORE_TILES
+            tiles = tiles_of(u)
+            s = tiles[0] % STORE_TILES
             nc.scalar.copy(
-                out=stage_of(u)[:, NORMED, s : s + UNIT, :], in_=live["keyvals", u][:, 1, :, :]
+                out=stage_of(tiles[0])[:, NORMED, s : s + len(tiles), :],
+                in_=live["keyvals", u][:, 1, :, :],
             )
 
         def normed_out(u, i, h):
-            s = (u * UNIT + i) % STORE_TILES
-            if h < QUERIES:
-                projected, g = live["queries", u][:, i, h, :], 0
-            else:
-                projected, g = live["keyvals", u][:, 0, i, :], 1
+            t = tiles_of(u)[i]
+            g = h // 2
             nc.vector.scalar_tensor_tensor(
-                out=stage_of(u)[:, h, s, :],
-                in0=projected,
+                out=stage_of(t)[:, h, t % STORE_TILES, :],
+                in0=projected(u, i, h),
                 scalar=live["rstd", u][:, i, h : h + 1],
                 in1=gain[:, g * HD : (g + 1) * HD],
                 op0=ALU.mult,
@@ -252,25 +273,27 @@ def tile_groupedqueryattention_pa_t_kernel(
             )
 
         def store(u):
-            first_tile = u * UNIT
-            stored = STORE_TILES
-            if first_tile >= TILES - 2 * STORE_TILES:
+            tiles = tiles_of(u)
+            end = tiles[-1] + 1
+            if tiles[0] < TILES - 2 * STORE_TILES:
+                stored = STORE_TILES
+            elif tiles[0] < TILES - STORE_TILES:
                 stored = STORE_TILES // 2
-            if first_tile >= TILES - STORE_TILES:
-                stored = UNIT
-            end_tile = first_tile + UNIT
-            if end_tile % stored == 0:
-                j0 = end_tile - stored
+            else:
+                stored = len(tiles)
+            if end % stored == 0:
+                j0 = end - stored
                 s0 = j0 % STORE_TILES
-                for h in range(HEADS):
+                stage = stage_of(j0)
+                for out_view, h in out_views:
                     nc.sync.dma_start(
-                        out=out_views[h][:, j0 : j0 + stored, :],
-                        in_=stage_of(u)[:, h, s0 : s0 + stored, :],
+                        out=out_view[:, j0:end, :], in_=stage[:, h, s0 : s0 + stored, :]
                     )
 
         for r in range(-3, UNITS + 1):
             this = 0 <= r < UNITS
             last = 0 <= r - 1 < UNITS
+            keys_on_scalar = r >= UNITS - SINGLES
             if r == 0:
                 spread_gains()
             if 0 <= r + 3 < UNITS:
@@ -279,23 +302,30 @@ def tile_groupedqueryattention_pa_t_kernel(
                 copy_out(r + 2)
             if 0 <= r + 1 < UNITS:
                 quantise(r + 1)
+                if r + 1 == 0:
+                    quantise_weights(slice(2, 4))
                 project(r + 1)
             if this:
-                squares(r)
-                key_stats(r)
+                sums = work.tile([P, len(tiles_of(r)), NORMED], F32)
+                live["sums", r] = sums
+                squares(r, list(range(NORMED if keys_on_scalar else QUERIES)))
+                if not keys_on_scalar:
+                    key_stats(r)
                 values_out(r)
+            query_outs = []
             if last:
-                for i in range(UNIT):
-                    normed_out(r - 1, 0, i)
-            if this:
+                query_outs = [(i, h) for i in range(len(tiles_of(r - 1))) for h in range(QUERIES)]
+            for i, h in query_outs[: len(query_outs) // 2]:
+                normed_out(r - 1, i, h)
+            if this and not keys_on_scalar:
                 key_mean_squares(r)
-            if last:
-                for i in range(UNIT):
-                    normed_out(r - 1, 1, i)
+            for i, h in query_outs[len(query_outs) // 2 :]:
+                normed_out(r - 1, i, h)
             if this:
-                key_sums(r)
+                if not keys_on_scalar:
+                    key_sums(r)
                 inverse_rms(r)
             if last:
-                for i in range(UNIT):
+                for i in range(len(tiles_of(r - 1))):
                     normed_out(r - 1, i, QUERIES)
                 store(r - 1)

@@ -28,7 +28,7 @@ SINGLES = 2
 UNIT_STARTS = list(range(0, TILES - SINGLES, UNIT)) + list(range(TILES - SINGLES, TILES))
 UNITS = len(UNIT_STARTS)
 WARM_COLS = 256
-WARM_UP = 10
+WARM_UP = 6
 LOAD_TILES = 8
 STORE_TILES = 8
 
@@ -63,8 +63,14 @@ def tile_groupedqueryattention_pa_t_kernel(
             for j in range(size):
                 x_words.append(x_chunk[:, j, :].bitcast(F32))
 
-        wq_raw = load_weight(Wq, QUERIES * HD, "wq_raw")
         load_x(UNIT)
+        wq_raw = load_weight(Wq, QUERIES * HD, "wq_raw")
+        gain_rows = consts.tile([P, 2 * HD], BF16)
+        nc.vector.memset(gain_rows[:], 0.0)
+        for g, w in enumerate((q_scale, k_scale)):
+            nc.sync.dma_start(
+                out=gain_rows[0:1, g * HD : (g + 1) * HD], in_=w.rearrange("(o d) -> o d", o=1)
+            )
         wk_raw = load_weight(Wk, HD, "wk_raw")
         wv_raw = load_weight(Wv, HD, "wv_raw")
         for size in [UNIT] * (LOAD_TILES // UNIT - 1) + [LOAD_TILES] * (TILES // LOAD_TILES - 1):
@@ -74,12 +80,6 @@ def tile_groupedqueryattention_pa_t_kernel(
         nc.vector.memset(eps[:], EPS)
         ones = consts.tile([P, WARM_COLS], BF16)
         nc.vector.memset(ones[:], 1.0)
-        gain_rows = consts.tile([P, 2 * HD], BF16)
-        nc.vector.memset(gain_rows[:], 0.0)
-        nc.scalar.dma_start(out=gain_rows[0:1, 0:HD], in_=q_scale.rearrange("(o d) -> o d", o=1))
-        nc.scalar.dma_start(
-            out=gain_rows[0:1, HD : 2 * HD], in_=k_scale.rearrange("(o d) -> o d", o=1)
-        )
         warm = consts.tile([P, 1], F32)
         nc.scalar.activation(out=warm[:], in_=eps[:], func=ACT.Abs_reciprocal_sqrt)
         ident = consts.tile([P, P], F32)
@@ -112,12 +112,12 @@ def tile_groupedqueryattention_pa_t_kernel(
 
         gain = consts.tile([P, 2 * HD], F32)
 
+        gain_ps = psum_acc.tile([P, N_OUT], F32, tag="kv")
+
         def spread_gains():
-            gain_ps = psum_acc.tile([P, N_OUT], F32, tag="kv")
             nc.tensor.matmul(
                 out=gain_ps[:, 0 : 2 * HD], lhsT=ones[:, 0:P], rhs=gain_rows[:], start=True, stop=True
             )
-            nc.vector.tensor_scalar_add(out=gain[:], in0=gain_ps[:, 0 : 2 * HD], scalar1=1.0)
 
         queries_out = out_0.flatten_outer_dims().rearrange("(h p j) d -> h p j d", h=2, p=P)
         out_views = [
@@ -172,31 +172,27 @@ def tile_groupedqueryattention_pa_t_kernel(
             codes, scales = live["codes", u]
             n_tiles = len(tiles_of(u))
             queries = psum_acc.tile([P, n_tiles, QUERIES, HD], F32, tag="q")
-            keyvals = psum_acc.tile([P, 2, n_tiles, HD], F32, tag="kv")
+            keyvals = psum_acc.tile([P, n_tiles, 2, HD], F32, tag="kv")
 
-            def multiply(out, i, first_col, cols):
-                nc.tensor.matmul_mx(
-                    out=out,
-                    lhsT=codes[:, i * P : (i + 1) * P].bitcast(FP8X4),
-                    lhsT_scale=scales[:, i * P : (i + 1) * P],
-                    rhs=w_codes[:, first_col : first_col + cols].bitcast(FP8X4),
-                    rhs_scale=w_scales[:, first_col : first_col + cols],
-                    start=True,
-                    stop=True,
-                )
-
-            for i in range(n_tiles):
-                multiply(queries[:, i, :, :].rearrange("p h d -> p (h d)"), i, 0, QUERIES * HD)
-            for i in range(n_tiles):
-                for g in range(2):
-                    multiply(keyvals[:, g, i, :], i, (QUERIES + g) * HD, HD)
+            for first_col, out in ((0, queries), (QUERIES * HD, keyvals)):
+                cols = slice(first_col, first_col + 2 * HD)
+                for i in range(n_tiles):
+                    nc.tensor.matmul_mx(
+                        out=out[:, i, :, :].rearrange("p h d -> p (h d)"),
+                        lhsT=codes[:, i * P : (i + 1) * P].bitcast(FP8X4),
+                        lhsT_scale=scales[:, i * P : (i + 1) * P],
+                        rhs=w_codes[:, cols].bitcast(FP8X4),
+                        rhs_scale=w_scales[:, cols],
+                        start=True,
+                        stop=True,
+                    )
             live["queries", u] = queries
             live["keyvals", u] = keyvals
 
         def projected(u, i, h):
             if h < QUERIES:
                 return live["queries", u][:, i, h, :]
-            return live["keyvals", u][:, h - QUERIES, i, :]
+            return live["keyvals", u][:, i, h - QUERIES, :]
 
         def squares(u, heads):
             n_tiles = len(tiles_of(u))
@@ -211,27 +207,24 @@ def tile_groupedqueryattention_pa_t_kernel(
                     )
 
         def key_stats(u):
-            n_tiles = len(tiles_of(u))
-            stats = work.tile([P, n_tiles, 2, 3], F32)
-            for i in range(n_tiles):
-                nc.vector.bn_stats(
-                    out=stats[:, i, :, :].rearrange("p e s -> p (e s)"),
-                    in_=projected(u, i, QUERIES),
-                )
+            stats = work.tile([P, UNIT, 3], F32)
+            nc.vector.bn_stats(
+                out=stats[:].rearrange("p i s -> p (i s)"),
+                in_=live["keyvals", u][:, :, 0, :].rearrange("p i d -> p d i"),
+            )
             live["stats", u] = stats
 
         def key_mean_squares(u):
-            means = live["stats", u][:].rearrange("p i e s -> p (i e) s")[:, :, 1]
+            means = live["stats", u][:, :, 1]
             nc.vector.scalar_tensor_tensor(
-                out=means, in0=means, scalar=HD / 2.0, in1=means, op0=ALU.mult, op1=ALU.mult
+                out=means, in0=means, scalar=float(HD), in1=means, op0=ALU.mult, op1=ALU.mult
             )
 
         def key_sums(u):
-            nc.vector.tensor_reduce(
+            nc.vector.tensor_add(
                 out=live["sums", u][:, :, QUERIES],
-                in_=live["stats", u][:, :, :, 1:3],
-                axis=mybir.AxisListType.XY,
-                op=ALU.add,
+                in0=live["stats", u][:, :, 1],
+                in1=live["stats", u][:, :, 2],
             )
 
         def inverse_rms(u):
@@ -257,7 +250,7 @@ def tile_groupedqueryattention_pa_t_kernel(
             s = tiles[0] % STORE_TILES
             nc.scalar.copy(
                 out=stage_of(tiles[0])[:, NORMED, s : s + len(tiles), :],
-                in_=live["keyvals", u][:, 1, :, :],
+                in_=live["keyvals", u][:, :, 1, :],
             )
 
         def normed_out(u, i, h):
@@ -294,16 +287,19 @@ def tile_groupedqueryattention_pa_t_kernel(
             this = 0 <= r < UNITS
             last = 0 <= r - 1 < UNITS
             keys_on_scalar = r >= UNITS - SINGLES
-            if r == 0:
-                spread_gains()
             if 0 <= r + 3 < UNITS:
                 transposes(r + 3)
+                if r + 3 == 0:
+                    spread_gains()
             if 0 <= r + 2 < UNITS:
                 copy_out(r + 2)
             if 0 <= r + 1 < UNITS:
                 quantise(r + 1)
                 if r + 1 == 0:
                     quantise_weights(slice(2, 4))
+                    nc.vector.tensor_scalar_add(
+                        out=gain[:], in0=gain_ps[:, 0 : 2 * HD], scalar1=1.0
+                    )
                 project(r + 1)
             if this:
                 sums = work.tile([P, len(tiles_of(r)), NORMED], F32)

@@ -207,24 +207,26 @@ def tile_groupedqueryattention_pa_t_kernel(
                     )
 
         def key_stats(u):
-            stats = work.tile([P, UNIT, 3], F32)
-            nc.vector.bn_stats(
-                out=stats[:].rearrange("p i s -> p (i s)"),
-                in_=live["keyvals", u][:, :, 0, :].rearrange("p i d -> p d i"),
-            )
+            stats = work.tile([P, UNIT, 2, 3], F32)
+            for i in range(UNIT):
+                nc.vector.bn_stats(
+                    out=stats[:, i, :, :].rearrange("p e s -> p (e s)"),
+                    in_=projected(u, i, QUERIES),
+                )
             live["stats", u] = stats
 
         def key_mean_squares(u):
-            means = live["stats", u][:, :, 1]
+            means = live["stats", u][:].rearrange("p i e s -> p (i e) s")[:, :, 1]
             nc.vector.scalar_tensor_tensor(
-                out=means, in0=means, scalar=float(HD), in1=means, op0=ALU.mult, op1=ALU.mult
+                out=means, in0=means, scalar=HD / 2.0, in1=means, op0=ALU.mult, op1=ALU.mult
             )
 
         def key_sums(u):
-            nc.vector.tensor_add(
+            nc.vector.tensor_reduce(
                 out=live["sums", u][:, :, QUERIES],
-                in0=live["stats", u][:, :, 1],
-                in1=live["stats", u][:, :, 2],
+                in_=live["stats", u][:, :, :, 1:3],
+                axis=mybir.AxisListType.XY,
+                op=ALU.add,
             )
 
         def inverse_rms(u):

from contextlib import ExitStack

import concourse.mybir as mybir
from concourse.masks import make_identity

F32 = mybir.dt.float32
BF16 = mybir.dt.bfloat16
U32 = mybir.dt.uint32
U8 = mybir.dt.uint8
FP8X4 = mybir.dt.float8_e4m3fn_x4
ACT = mybir.ActivationFunctionType
ALU = mybir.AluOpType

P = 128
TOKENS = 8192
K = 512
PACK = 4
HD = 128
HEADS = 4
NORMED = 3
QUERIES = 2
N_OUT = HEADS * HD
EPS = 1e-6

TILES = TOKENS // P
UNIT = 2
SINGLES = 2
UNIT_STARTS = list(range(0, TILES - SINGLES, UNIT)) + list(range(TILES - SINGLES, TILES))
UNITS = len(UNIT_STARTS)
WARM_COLS = 256
WARM_UP = 6
LOAD_TILES = 8
STORE_TILES = 8

FLOPS = 2 * TOKENS * K * N_OUT


def tile_groupedqueryattention_pa_t_kernel(
    tc, x, Wq, Wk, Wv, q_scale, k_scale, out_0, out_1, out_2
):
    nc = tc.nc
    with ExitStack() as ctx:
        ctx.enter_context(tc.manual_schedule())
        consts = ctx.enter_context(tc.tile_pool(name="consts", bufs=1))
        xin = ctx.enter_context(tc.tile_pool(name="xin", bufs=1))
        work = ctx.enter_context(tc.tile_pool(name="work", bufs=3))
        stages = ctx.enter_context(tc.tile_pool(name="stages", bufs=6))
        psum_xt = ctx.enter_context(tc.psum_pool(name="psum_xt", bufs=2))
        psum_acc = ctx.enter_context(tc.psum_pool(name="psum_acc", bufs=3))

        def load_weight(w_dram, cols, name):
            w_raw = consts.tile([P, PACK, cols], BF16, name=name)
            nc.sync.dma_start(out=w_raw[:], in_=w_dram.rearrange("(p t) c -> p t c", t=PACK))
            return w_raw

        x_view = x.flatten_outer_dims().rearrange("(p j) k -> p j k", p=P)
        x_words = []

        def load_x(size):
            j0 = len(x_words)
            x_chunk = xin.tile([P, size, K], BF16, name="x_chunk%d" % j0)
            nc.sync.dma_start(out=x_chunk[:], in_=x_view[:, j0 : j0 + size, :])
            for j in range(size):
                x_words.append(x_chunk[:, j, :].bitcast(F32))

        load_x(UNIT)
        wq_raw = load_weight(Wq, QUERIES * HD, "wq_raw")
        gain_rows = consts.tile([P, 2 * HD], BF16)
        nc.vector.memset(gain_rows[:], 0.0)
        for g, w in enumerate((q_scale, k_scale)):
            nc.sync.dma_start(
                out=gain_rows[0:1, g * HD : (g + 1) * HD], in_=w.rearrange("(o d) -> o d", o=1)
            )
        wk_raw = load_weight(Wk, HD, "wk_raw")
        wv_raw = load_weight(Wv, HD, "wv_raw")
        for size in [UNIT] * (LOAD_TILES // UNIT - 1) + [LOAD_TILES] * (TILES // LOAD_TILES - 1):
            load_x(size)

        eps = consts.tile([P, 1], F32)
        nc.vector.memset(eps[:], EPS)
        ones = consts.tile([P, WARM_COLS], BF16)
        nc.vector.memset(ones[:], 1.0)
        warm = consts.tile([P, 1], F32)
        nc.scalar.activation(out=warm[:], in_=eps[:], func=ACT.Abs_reciprocal_sqrt)
        ident = consts.tile([P, P], F32)
        make_identity(nc, ident[:])

        w_grouped = consts.tile([P, N_OUT, PACK], BF16, align_bytes=64)
        w_codes = consts.tile([P, N_OUT], U32, align_bytes=64)
        w_scales = consts.tile([P, N_OUT], U8, align_bytes=64)

        def regroup(copy, w_raw, h):
            first = h * HD if h < QUERIES else 0
            copy(
                out=w_grouped[:, h * HD : (h + 1) * HD, :],
                in_=w_raw[:, :, first : first + HD].rearrange("p t c -> p c t"),
            )

        def quantise_weights(heads):
            cols = slice(heads.start * HD, heads.stop * HD)
            nc.vector.quantize_mx(
                out=w_codes[:, cols].bitcast(FP8X4),
                scales=w_scales[:, cols],
                in_=w_grouped[:, cols, :].rearrange("p c t -> p (c t)"),
            )

        regroup(nc.vector.tensor_copy, wq_raw, 0)
        regroup(nc.scalar.copy, wq_raw, 1)
        regroup(nc.vector.tensor_copy, wk_raw, 2)
        quantise_weights(slice(0, 2))
        regroup(nc.vector.tensor_copy, wv_raw, 3)

        gain = consts.tile([P, 2 * HD], F32)

        gain_ps = psum_acc.tile([P, N_OUT], F32, tag="kv")

        def spread_gains():
            nc.tensor.matmul(
                out=gain_ps[:, 0 : 2 * HD], lhsT=ones[:, 0:P], rhs=gain_rows[:], start=True, stop=True
            )

        queries_out = out_0.flatten_outer_dims().rearrange("(h p j) d -> h p j d", h=2, p=P)
        out_views = [
            (out_2.flatten_outer_dims().rearrange("(p j) d -> p j d", p=P), NORMED),
            (queries_out[0], 0),
            (queries_out[1], 1),
            (out_1.flatten_outer_dims().rearrange("(p j) d -> p j d", p=P), QUERIES),
        ]

        def tiles_of(u):
            end = UNIT_STARTS[u + 1] if u + 1 < UNITS else TILES
            return list(range(UNIT_STARTS[u], end))

        def keep_warm(xt):
            nc.tensor.matmul(
                out=xt[:].rearrange("p i h n -> p (i h n)")[:, 0:WARM_COLS],
                lhsT=ones[:, 0:P],
                rhs=ones[:],
                start=True,
                stop=True,
            )

        live = {}

        def transposes(u):
            tiles = tiles_of(u)
            xt = psum_xt.tile([P, len(tiles), 2, P], F32)
            for n in range(WARM_UP if u == 0 else 1):
                keep_warm(xt)
            for i, t in enumerate(tiles):
                for h in range(2):
                    nc.tensor.transpose(xt[:, i, h, :], x_words[t][:, h : 2 * P : 2], ident[:])
            live["xt", u] = xt

        def copy_out(u):
            n_tiles = len(tiles_of(u))
            grouped = work.tile([P, n_tiles * P * PACK], BF16, align_bytes=64)
            interleaved = grouped[:].bitcast(F32).rearrange("p (i n h) -> p i n h", i=n_tiles, h=2)
            nc.scalar.copy(out=interleaved, in_=live["xt", u][:].rearrange("p i h n -> p i n h"))
            live["grouped", u] = grouped

        def quantise(u):
            cols = len(tiles_of(u)) * P
            codes = work.tile([P, cols], U32, align_bytes=64)
            scales = work.tile([P, cols], U8, align_bytes=64)
            nc.vector.quantize_mx(
                out=codes[:].bitcast(FP8X4), scales=scales[:], in_=live["grouped", u][:]
            )
            live["codes", u] = (codes, scales)

        def project(u):
            codes, scales = live["codes", u]
            n_tiles = len(tiles_of(u))
            queries = psum_acc.tile([P, n_tiles, QUERIES, HD], F32, tag="q")
            keyvals = psum_acc.tile([P, n_tiles, 2, HD], F32, tag="kv")

            for first_col, out in ((0, queries), (QUERIES * HD, keyvals)):
                cols = slice(first_col, first_col + 2 * HD)
                for i in range(n_tiles):
                    nc.tensor.matmul_mx(
                        out=out[:, i, :, :].rearrange("p h d -> p (h d)"),
                        lhsT=codes[:, i * P : (i + 1) * P].bitcast(FP8X4),
                        lhsT_scale=scales[:, i * P : (i + 1) * P],
                        rhs=w_codes[:, cols].bitcast(FP8X4),
                        rhs_scale=w_scales[:, cols],
                        start=True,
                        stop=True,
                    )
            live["queries", u] = queries
            live["keyvals", u] = keyvals

        def projected(u, i, h):
            if h < QUERIES:
                return live["queries", u][:, i, h, :]
            return live["keyvals", u][:, i, h - QUERIES, :]

        def squares(u, heads):
            n_tiles = len(tiles_of(u))
            squared = work.tile([P, n_tiles, len(heads), HD], F32)
            for i in range(n_tiles):
                for c, h in enumerate(heads):
                    nc.scalar.activation(
                        out=squared[:, i, c, :],
                        in_=projected(u, i, h),
                        func=ACT.Square,
                        accum_out=live["sums", u][:, i, h : h + 1],
                    )

        def key_stats(u):
            stats = work.tile([P, UNIT, 2, 3], F32)
            for i in range(UNIT):
                nc.vector.bn_stats(
                    out=stats[:, i, :, :].rearrange("p e s -> p (e s)"),
                    in_=projected(u, i, QUERIES),
                )
            live["stats", u] = stats

        def key_mean_squares(u):
            means = live["stats", u][:].rearrange("p i e s -> p (i e) s")[:, :, 1]
            nc.vector.scalar_tensor_tensor(
                out=means, in0=means, scalar=HD / 2.0, in1=means, op0=ALU.mult, op1=ALU.mult
            )

        def key_sums(u):
            nc.vector.tensor_reduce(
                out=live["sums", u][:, :, QUERIES],
                in_=live["stats", u][:, :, :, 1:3],
                axis=mybir.AxisListType.XY,
                op=ALU.add,
            )

        def inverse_rms(u):
            rstd = work.tile([P, len(tiles_of(u)), NORMED], F32)
            nc.scalar.activation(
                out=rstd[:],
                in_=live["sums", u][:],
                func=ACT.Abs_reciprocal_sqrt,
                scale=1.0 / HD,
                bias=eps[:],
            )
            live["rstd", u] = rstd

        def stage_of(t):
            key = ("stage", t // STORE_TILES)
            if key not in live:
                stage = stages.tile([P, HEADS, STORE_TILES, HD], F32)
                live[key] = stage
            return live[key]

        def values_out(u):
            tiles = tiles_of(u)
            s = tiles[0] % STORE_TILES
            nc.scalar.copy(
                out=stage_of(tiles[0])[:, NORMED, s : s + len(tiles), :],
                in_=live["keyvals", u][:, :, 1, :],
            )

        def normed_out(u, i, h):
            t = tiles_of(u)[i]
            g = h // 2
            nc.vector.scalar_tensor_tensor(
                out=stage_of(t)[:, h, t % STORE_TILES, :],
                in0=projected(u, i, h),
                scalar=live["rstd", u][:, i, h : h + 1],
                in1=gain[:, g * HD : (g + 1) * HD],
                op0=ALU.mult,
                op1=ALU.mult,
            )

        def store(u):
            tiles = tiles_of(u)
            end = tiles[-1] + 1
            if tiles[0] < TILES - 2 * STORE_TILES:
                stored = STORE_TILES
            elif tiles[0] < TILES - STORE_TILES:
                stored = STORE_TILES // 2
            else:
                stored = len(tiles)
            if end % stored == 0:
                j0 = end - stored
                s0 = j0 % STORE_TILES
                stage = stage_of(j0)
                for out_view, h in out_views:
                    nc.sync.dma_start(
                        out=out_view[:, j0:end, :], in_=stage[:, h, s0 : s0 + stored, :]
                    )

        for r in range(-3, UNITS + 1):
            this = 0 <= r < UNITS
            last = 0 <= r - 1 < UNITS
            keys_on_scalar = r >= UNITS - SINGLES
            if 0 <= r + 3 < UNITS:
                transposes(r + 3)
                if r + 3 == 0:
                    spread_gains()
            if 0 <= r + 2 < UNITS:
                copy_out(r + 2)
            if 0 <= r + 1 < UNITS:
                quantise(r + 1)
                if r + 1 == 0:
                    quantise_weights(slice(2, 4))
                    nc.vector.tensor_scalar_add(
                        out=gain[:], in0=gain_ps[:, 0 : 2 * HD], scalar1=1.0
                    )
                project(r + 1)
            if this:
                sums = work.tile([P, len(tiles_of(r)), NORMED], F32)
                live["sums", r] = sums
                squares(r, list(range(NORMED if keys_on_scalar else QUERIES)))
                if not keys_on_scalar:
                    key_stats(r)
                values_out(r)
            query_outs = []
            if last:
                query_outs = [(i, h) for i in range(len(tiles_of(r - 1))) for h in range(QUERIES)]
            for i, h in query_outs[: len(query_outs) // 2]:
                normed_out(r - 1, i, h)
            if this and not keys_on_scalar:
                key_mean_squares(r)
            for i, h in query_outs[len(query_outs) // 2 :]:
                normed_out(r - 1, i, h)
            if this:
                if not keys_on_scalar:
                    key_sums(r)
                inverse_rms(r)
            if last:
                for i in range(len(tiles_of(r - 1))):
                    normed_out(r - 1, i, QUERIES)
                store(r - 1)
